import numpy as np
import ml_dtypes


def mxq(x, axis, fmt="e4m3"):
    dtype, down = {"e4m3": (ml_dtypes.float8_e4m3fn, 7), "e5m2": (ml_dtypes.float8_e5m2, 14)}[fmt]
    v = np.moveaxis(np.asarray(x, np.float32).astype(ml_dtypes.bfloat16).astype(np.float64), axis, -1)
    blocks = v.reshape(v.shape[:-1] + (-1, 32))
    amax = np.abs(blocks).max(-1, keepdims=True)
    byte = np.maximum(np.where(amax > 0, np.frexp(amax)[1] - 1 + 127, 0) - down, 1)
    scale = np.exp2(byte - 127.0)
    codes = (blocks / scale).astype(np.float32).astype(dtype).astype(np.float64)
    return np.moveaxis((codes * scale).reshape(v.shape), -1, axis)


WIDE = False


def mx_kscale(k):
    if not WIDE:
        return np.ones(k)
    levels = np.array([10, -10, 5, -5, 0])
    a = np.random.permutation(np.resize(levels, k // 512 * 4)).reshape(k // 512, 4)
    idx = np.arange(k)
    return np.exp2(a[idx // 512, idx % 128 // 32])


BF16 = ml_dtypes.bfloat16


def bf(x):
    return np.asarray(x, np.float32).astype(BF16)


def f64(x):
    return np.asarray(x).astype(np.float64)


B, NB, IBS, BS = 256, 8, 512, 512


def sigmoid(v):
    return 1.0 / (1.0 + np.exp(-v))


def setup_inputs():
    s = mx_kscale(IBS)
    return {
        "x": bf((np.random.standard_normal((B, NB, IBS)) * s).reshape(B, NB * IBS)),
        "h": bf(np.random.standard_normal((B, NB * BS))),
        "W_ih": bf(np.random.standard_normal((NB, 3 * BS, IBS)) / np.sqrt(IBS) / s),
        "W_hh": bf(np.random.standard_normal((NB, 3 * BS, BS)) / np.sqrt(BS)),
        "b_ih": bf(np.random.standard_normal((NB, 3 * BS)) * 0.2),
        "b_hh": bf(np.random.standard_normal((NB, 3 * BS)) * 0.2),
    }


def reference(x, h, W_ih, W_hh, b_ih, b_hh):
    xb = f64(x).reshape(B, NB, IBS)
    hb = f64(h).reshape(B, NB, BS)
    gi = (mxq(xb, 2, "e4m3").transpose(1, 0, 2) @ mxq(f64(W_ih), 2, "e4m3").transpose(0, 2, 1)).transpose(1, 0, 2) + f64(b_ih)
    gh = (mxq(hb, 2, "e4m3").transpose(1, 0, 2) @ mxq(f64(W_hh), 2, "e4m3").transpose(0, 2, 1)).transpose(1, 0, 2) + f64(b_hh)
    i_r, i_z, i_n = np.split(gi, 3, axis=-1)
    h_r, h_z, h_n = np.split(gh, 3, axis=-1)
    r = sigmoid(i_r + h_r)
    z = sigmoid(i_z + h_z)
    n_gate = np.tanh(i_n + r * h_n)
    new_h = n_gate + z * (hb - n_gate)
    return new_h.reshape(B, NB * BS)

@@ -1,0 +1,352 @@
+from contextlib import ExitStack
+
+import concourse.mybir as mybir
+from concourse.masks import make_identity
+
+F32 = mybir.dt.float32
+BF16 = mybir.dt.bfloat16
+U32 = mybir.dt.uint32
+U8 = mybir.dt.uint8
+FP8X4 = mybir.dt.float8_e4m3fn_x4
+ACT = mybir.ActivationFunctionType
+ALU = mybir.AluOpType
+
+P = 128
+NB = 8
+K = 512
+BATCH = 256
+FLOPS = 2 * BATCH * (3 * K) * K * NB * 2
+
+MANUAL = True
+EV_R = "ssss"
+EV_Z = "ssss"
+EV_N = "sssv"
+EV_A = "vvss"
+
+
+def tile_blockdiagonalgru_kernel(tc, x, h, W_ih, W_hh, b_ih, b_hh, out):
+    nc = tc.nc
+    with ExitStack() as ctx:
+        const = ctx.enter_context(tc.tile_pool(name="const", bufs=1))
+        wpool = ctx.enter_context(tc.tile_pool(name="wpool", bufs=3))
+        grp = ctx.enter_context(tc.tile_pool(name="grp", bufs=4))
+        cod = ctx.enter_context(tc.tile_pool(name="cod", bufs=4))
+        epi = ctx.enter_context(tc.tile_pool(name="epi", bufs=2))
+        psT = ctx.enter_context(tc.psum_pool(name="psT", bufs=4))
+        psM = ctx.enter_context(tc.psum_pool(name="psM", bufs=4))
+        if MANUAL:
+            ctx.enter_context(tc.manual_schedule())
+
+        x_view = x.rearrange("(a p) c -> p a c", p=P)
+        h_view = h.rearrange("(a p) c -> p a c", p=P)
+        out_view = out.rearrange("(a b) c -> b a c", b=P)
+        w_view = [
+            W_ih.rearrange("n (s p e) k -> n p s (e k)", p=P, e=2),
+            W_hh.rearrange("n (s p e) k -> n p s (e k)", p=P, e=2),
+        ]
+
+        ident = const.tile([P, P], F32, name="ident")
+        make_identity(nc, ident[:])
+        groups = [(0, 1), (1, 2), (2, 4), (4, 8)]
+        xh_raw = {}
+        xh_words = {}
+        for n0, n1 in groups:
+            xt = const.tile([P, 2, (n1 - n0) * K], BF16, name="x%d" % n0)
+            ht = const.tile([P, 2, (n1 - n0) * K], BF16, name="h%d" % n0)
+            xh_raw[n0] = (xt, ht)
+            for n in range(n0, n1):
+                xh_words[n] = [
+                    xt[:].bitcast(F32)[:, :, (n - n0) * 256:(n - n0 + 1) * 256],
+                    ht[:].bitcast(F32)[:, :, (n - n0) * 256:(n - n0 + 1) * 256],
+                ]
+        braw = [const.tile([P, 256], BF16, name="braw%d" % m) for m in range(2)]
+        bias_f = const.tile([P, 2, P, 2], F32, name="bias_f")
+        brz = const.tile([P, 48, 2], F32, name="brz")
+
+        st = {}
+
+        def evac(eng, dst, src):
+            if eng == "s":
+                nc.scalar.copy(out=dst, in_=src)
+            else:
+                nc.vector.tensor_copy(out=dst, in_=src)
+
+        def load_xh(n0, n1):
+            cols = slice(n0 * K, n1 * K)
+            nc.sync.dma_start(out=xh_raw[n0][0][:], in_=x_view[:, :, cols])
+            nc.sync.dma_start(out=xh_raw[n0][1][:], in_=h_view[:, :, cols])
+
+        def w_tile(n, m):
+            if ("w", n, m) not in st:
+                st["w", n, m] = wpool.tile([P, 6, 2 * K], BF16, name="wraw%d" % m)
+            return st["w", n, m]
+
+        def load_w(n, m, s0, s1):
+            nc.sync.dma_start(out=w_tile(n, m)[:, s0:s1, :], in_=w_view[m][n, :, s0:s1, :])
+
+        def prep_bias():
+            for m, b in enumerate((b_ih, b_hh)):
+                nc.gpsimd.memset(braw[m][:], 0.0)
+                nc.gpsimd.dma_start(out=braw[m][0:48, :], in_=b.rearrange("n (s w) -> (n s) w", w=256))
+
+        def bias_transpose():
+            bps = psT.tile([P, 512], F32, name="tp", tag="T")
+            for m in range(2):
+                nc.tensor.transpose(bps[:, m * P:(m + 1) * P], braw[m][:].bitcast(F32), ident[:])
+            nc.vector.tensor_copy(out=bias_f[:].rearrange("p m r e -> p (m r e)"), in_=bps[:, 0:2 * P].bitcast(BF16))
+            nc.vector.tensor_tensor(out=brz[:], in0=bias_f[:, 0, 0:48, :], in1=bias_f[:, 1, 0:48, :], op=ALU.add)
+
+        def t_chunk(key, srcs):
+            banks = []
+            for b in range(2):
+                tp = psT.tile([P, 512], F32, name="tp", tag="T")
+                for i in range(2):
+                    for kv in range(2):
+                        c0 = (i * 2 + kv) * P
+                        nc.tensor.transpose(tp[:, c0:c0 + P], srcs[2 * b + i][:, kv * P:(kv + 1) * P], ident[:])
+                banks.append(tp)
+            st["tb", key] = banks
+
+        def t_w(n, m, g):
+            ww = w_tile(n, m)[:].bitcast(F32)
+            t_chunk(("w", n, m, g), [ww[:, g * 2 + t // 2, (t % 2) * 256:(t % 2) * 256 + 256] for t in range(4)])
+
+        def t_xh(n):
+            t_chunk(("xh", n), [xh_words[n][q][:, a, :] for q in range(2) for a in range(2)])
+
+        def e_bank(key, b, eng):
+            if ("g", key) not in st:
+                tag = "gx" if key[0] == "xh" else "gw"
+                st["g", key] = grp.tile([P, 4 * K], BF16, name=tag, bufs=4, align_bytes=64)
+            g32 = st["g", key][:].bitcast(F32)
+            evac(
+                eng,
+                g32[:, b * 512:(b + 1) * 512].rearrange("p (i r v) -> p i r v", i=2, v=2),
+                st["tb", key][b][:].rearrange("p (i v r) -> p i r v", i=2, v=2),
+            )
+
+        def q_w(n, m, g):
+            if ("wc", n, g) not in st:
+                st["wc", n, g] = cod.tile([P, 2, 512], U32, name="wc", align_bytes=64)
+                st["ws", n, g] = cod.tile([P, 2, 512], U8, name="ws", align_bytes=64)
+            nc.vector.quantize_mx(
+                out=st["wc", n, g][:, m, :].bitcast(FP8X4), scales=st["ws", n, g][:, m, :], in_=st["g", ("w", n, m, g)][:]
+            )
+
+        def q_xh(n):
+            st["xc", n] = cod.tile([P, 512], U32, name="xc", bufs=3, align_bytes=64)
+            st["xs", n] = cod.tile([P, 512], U8, name="xs", bufs=3, align_bytes=64)
+            nc.vector.quantize_mx(out=st["xc", n][:].bitcast(FP8X4), scales=st["xs", n][:], in_=st["g", ("xh", n)][:])
+
+        def mx(n, g, m, t, dst, start, stop):
+            nc.tensor.matmul_mx(
+                out=dst,
+                lhsT=st["wc", n, g][:, m, t * P:(t + 1) * P].bitcast(FP8X4),
+                lhsT_scale=st["ws", n, g][:, m, t * P:(t + 1) * P],
+                rhs=st["xc", n][:, m * BATCH:(m + 1) * BATCH].bitcast(FP8X4),
+                rhs_scale=st["xs", n][:, m * BATCH:(m + 1) * BATCH],
+                start=start,
+                stop=stop,
+            )
+
+        def mx_rz(n, g):
+            banks = []
+            for ju in range(2):
+                mp = psM.tile([P, 512], F32, name="mp", tag="M")
+                for je in range(2):
+                    for m in range(2):
+                        mx(n, g, m, 2 * ju + je, mp[:, je * BATCH:(je + 1) * BATCH], m == 0, m == 1)
+                banks.append(mp)
+            st["m", n, g] = banks
+
+        def mx_n(n, ju):
+            pair = []
+            for m in (1, 0):
+                mp = psM.tile([P, 512], F32, name="mp", tag="M")
+                for je in range(2):
+                    mx(n, 2, m, 2 * ju + je, mp[:, je * BATCH:(je + 1) * BATCH], True, True)
+                pair.append(mp)
+            st["mn", n, ju] = pair
+
+        def sig(n, g):
+            dst = epi.tile([P, 4, BATCH], F32, name="gate%d" % g, bufs=2 + g)
+            st["gate", n, g] = dst
+            for t in range(4):
+                nc.scalar.activation(
+                    out=dst[:, t, :],
+                    in_=st["m", n, g][t // 2][:, (t % 2) * BATCH:(t % 2 + 1) * BATCH],
+                    func=ACT.Sigmoid,
+                    bias=brz[:, n * 6 + g * 2 + t // 2, t % 2:t % 2 + 1],
+                    scale=1.0,
+                )
+
+        def n_pre(n, ju):
+            y = epi.tile([P, 2, BATCH], F32, name="y", bufs=3)
+            st["y", n, ju] = y
+            hn, xn = st["mn", n, ju]
+            for je in range(2):
+                nc.vector.scalar_tensor_tensor(
+                    out=y[:, je, :],
+                    in0=hn[:, je * BATCH:(je + 1) * BATCH],
+                    scalar=bias_f[:, 1, n * 6 + 4 + ju, je:je + 1],
+                    in1=st["gate", n, 0][:, 2 * ju + je, :],
+                    op0=ALU.add,
+                    op1=ALU.mult,
+                )
+            yf = y[:].rearrange("p e b -> p (e b)")
+            nc.vector.tensor_tensor(out=yf, in0=xn[:], in1=yf, op=ALU.add)
+
+        def n_tanh(n, ju):
+            c = epi.tile([P, 2, BATCH], F32, name="c", bufs=4)
+            st["c", n, ju] = c
+            for je in range(2):
+                nc.scalar.activation(
+                    out=c[:, je, :],
+                    in_=st["y", n, ju][:, je, :],
+                    func=ACT.Tanh,
+                    bias=bias_f[:, 0, n * 6 + 4 + ju, je:je + 1],
+                    scale=1.0,
+                )
+            pending.extend([(n, ju, 0), (n, ju, 1), (n, ju, 2)])
+
+        def blend(n, ju, step):
+            c = st["c", n, ju]
+            if step == 0:
+                d = epi.tile([P, 2, BATCH], F32, name="d", bufs=3)
+                st["d", n, ju] = d
+                h_t = st["g", ("xh", n)][:, 2 * K:4 * K].rearrange("p (b t) -> p t b", t=4)[:, 2 * ju:2 * ju + 2, :]
+                nc.vector.tensor_tensor(out=d[:], in0=h_t, in1=c[:], op=ALU.subtract)
+            elif step == 1:
+                d = st["d", n, ju]
+                nc.vector.tensor_tensor(out=d[:], in0=d[:], in1=st["gate", n, 1][:, 2 * ju:2 * ju + 2, :], op=ALU.mult)
+            else:
+                o = epi.tile([P, 2, BATCH], F32, name="o", bufs=6)
+                st["o", n, ju] = o
+                nc.vector.tensor_tensor(out=o[:], in0=st["d", n, ju][:], in1=c[:], op=ALU.add)
+
+        def t_out(n):
+            banks = []
+            for a in range(2):
+                tp = psT.tile([P, 512], F32, name="tp", tag="T")
+                for t in range(4):
+                    nc.tensor.transpose(tp[:, t * P:(t + 1) * P], st["o", n, t // 2][:, t % 2, a * P:(a + 1) * P], ident[:])
+                banks.append(tp)
+            st["ot", n] = banks
+
+        def e_out(n, engs):
+            osb = epi.tile([P, 2, K], F32, name="osb")
+            for a in range(2):
+                evac(
+                    engs[a],
+                    osb[:, a, :].rearrange("b (ju p je) -> b ju p je", ju=2, je=2),
+                    st["ot", n][a][:].rearrange("b (ju je p) -> b ju p je", ju=2, je=2),
+                )
+            nc.sync.dma_start(out=out_view[:, :, n * K:(n + 1) * K], in_=osb[:])
+
+        pending = []
+        blended = []
+
+        cursor = [0, 0]
+
+        def bl(count=1):
+            for i in range(count):
+                if cursor[0] < len(pending):
+                    n, ju, step = pending[cursor[0]]
+                    cursor[0] = cursor[0] + 1
+                    blend(n, ju, step)
+                    if ju == 1 and step == 2:
+                        blended.append(n)
+
+        def load_block(n):
+            for g in range(3):
+                load_w(n, 0, 2 * g, 2 * g + 2)
+                load_w(n, 1, 2 * g, 2 * g + 2)
+
+        def t_pair(n, g):
+            t_w(n, 0, g)
+            t_w(n, 1, g)
+
+        def e_pair(n, g, banks, engs):
+            for b in banks:
+                e_bank(("w", n, b // 2, g), b % 2, engs[b])
+
+        load_xh(0, 1)
+        prep_bias()
+        load_block(0)
+        load_xh(1, 2)
+        load_block(1)
+        load_xh(2, 4)
+        load_block(2)
+        load_xh(4, 8)
+
+        t_xh(0)
+        e_bank(("xh", 0), 0, "s")
+        e_bank(("xh", 0), 1, "v")
+        bias_transpose()
+        q_xh(0)
+
+        for n in range(NB + 2):
+            cur = n < NB
+            prev = 1 <= n <= NB
+            if cur:
+                t_pair(n, 0)
+            if prev:
+                n_pre(n - 1, 0)
+            if cur:
+                e_pair(n, 0, (0, 1, 2, 3), EV_R)
+            bl()
+            if cur:
+                q_w(n, 0, 0)
+            bl()
+            if cur:
+                q_w(n, 1, 0)
+            if prev:
+                n_tanh(n - 1, 0)
+                mx_n(n - 1, 1)
+            if cur:
+                t_pair(n, 1)
+            if prev:
+                n_pre(n - 1, 1)
+            if cur:
+                e_pair(n, 1, (0, 1, 2, 3), EV_Z)
+            if prev:
+                n_tanh(n - 1, 1)
+            if cur:
+                mx_rz(n, 0)
+                q_w(n, 0, 1)
+            bl()
+            if cur:
+                q_w(n, 1, 1)
+            bl()
+            if cur:
+                t_pair(n, 2)
+                if n + 3 < NB:
+                    load_block(n + 3)
+                e_pair(n, 2, (0, 1), EV_N)
+                sig(n, 0)
+                e_pair(n, 2, (2, 3), EV_N)
+                mx_rz(n, 1)
+            bl()
+            if cur:
+                q_w(n, 0, 2)
+            bl()
+            if cur:
+                q_w(n, 1, 2)
+            if n + 1 < NB:
+                t_xh(n + 1)
+            done = blended[cursor[1]:]
+            cursor[1] = len(blended)
+            for m in done:
+                t_out(m)
+            if cur:
+                sig(n, 1)
+            if n + 1 < NB:
+                e_bank(("xh", n + 1), 0, EV_A[0])
+                e_bank(("xh", n + 1), 1, EV_A[1])
+            for m in done:
+                e_out(m, EV_A[2:4])
+            if cur:
+                mx_n(n, 0)
+            bl()
+            if n + 1 < NB:
+                q_xh(n + 1)

@@ -86,8 +86,8 @@ def tile_blockdiagonalgru_kernel(tc, x, h, W_ih, W_hh, b_ih, b_hh, out):
 
         def prep_bias():
             for m, b in enumerate((b_ih, b_hh)):
-                nc.gpsimd.memset(braw[m][:], 0.0)
-                nc.gpsimd.dma_start(out=braw[m][0:48, :], in_=b.rearrange("n (s w) -> (n s) w", w=256))
+                nc.vector.memset(braw[m][:], 0.0)
+                nc.scalar.dma_start(out=braw[m][0:48, :], in_=b.rearrange("n (s w) -> (n s) w", w=256))
 
         def bias_transpose():
             bps = psT.tile([P, 512], F32, name="tp", tag="T")
@@ -282,7 +282,6 @@ def tile_blockdiagonalgru_kernel(tc, x, h, W_ih, W_hh, b_ih, b_hh, out):
         t_xh(0)
         e_bank(("xh", 0), 0, "s")
         e_bank(("xh", 0), 1, "v")
-        bias_transpose()
         q_xh(0)
 
         for n in range(NB + 2):
@@ -318,6 +317,8 @@ def tile_blockdiagonalgru_kernel(tc, x, h, W_ih, W_hh, b_ih, b_hh, out):
             if cur:
                 q_w(n, 1, 1)
             bl()
+            if n == 0:
+                bias_transpose()
             if cur:
                 t_pair(n, 2)
                 if n + 3 < NB:

@@ -18,7 +18,7 @@ BATCH = 256
 FLOPS = 2 * BATCH * (3 * K) * K * NB * 2
 
 MANUAL = True
-EV_R = "ssss"
+EV_R = "sssv"
 EV_Z = "ssss"
 EV_N = "sssv"
 EV_A = "vvss"
@@ -197,7 +197,7 @@ def tile_blockdiagonalgru_kernel(tc, x, h, W_ih, W_hh, b_ih, b_hh, out):
             nc.vector.tensor_tensor(out=yf, in0=xn[:], in1=yf, op=ALU.add)
 
         def n_tanh(n, ju):
-            c = epi.tile([P, 2, BATCH], F32, name="c", bufs=4)
+            c = epi.tile([P, 2, BATCH], F32, name="c", bufs=6)
             st["c", n, ju] = c
             for je in range(2):
                 nc.scalar.activation(
@@ -207,29 +207,34 @@ def tile_blockdiagonalgru_kernel(tc, x, h, W_ih, W_hh, b_ih, b_hh, out):
                     bias=bias_f[:, 0, n * 6 + 4 + ju, je:je + 1],
                     scale=1.0,
                 )
-            pending.extend([(n, ju, 0), (n, ju, 1), (n, ju, 2)])
+            pending.extend([(n, ju, 0), (n, ju, 1)])
 
         def blend(n, ju, step):
             c = st["c", n, ju]
             if step == 0:
-                d = epi.tile([P, 2, BATCH], F32, name="d", bufs=3)
+                d = epi.tile([P, 2, BATCH], F32, name="d", bufs=6)
                 st["d", n, ju] = d
                 h_t = st["g", ("xh", n)][:, 2 * K:4 * K].rearrange("p (b t) -> p t b", t=4)[:, 2 * ju:2 * ju + 2, :]
                 nc.vector.tensor_tensor(out=d[:], in0=h_t, in1=c[:], op=ALU.subtract)
-            elif step == 1:
+            else:
                 d = st["d", n, ju]
                 nc.vector.tensor_tensor(out=d[:], in0=d[:], in1=st["gate", n, 1][:, 2 * ju:2 * ju + 2, :], op=ALU.mult)
-            else:
-                o = epi.tile([P, 2, BATCH], F32, name="o", bufs=6)
-                st["o", n, ju] = o
-                nc.vector.tensor_tensor(out=o[:], in0=st["d", n, ju][:], in1=c[:], op=ALU.add)
+
 
         def t_out(n):
             banks = []
             for a in range(2):
                 tp = psT.tile([P, 512], F32, name="tp", tag="T")
                 for t in range(4):
-                    nc.tensor.transpose(tp[:, t * P:(t + 1) * P], st["o", n, t // 2][:, t % 2, a * P:(a + 1) * P], ident[:])
+                    for i, term in enumerate(("c", "d")):
+                        nc.tensor.matmul(
+                            out=tp[:, t * P:(t + 1) * P],
+                            lhsT=st[term, n, t // 2][:, t % 2, a * P:(a + 1) * P],
+                            rhs=ident[:],
+                            start=(i == 0),
+                            stop=(i == 1),
+                            is_transpose=True,
+                        )
                 banks.append(tp)
             st["ot", n] = banks
 
@@ -254,7 +259,7 @@ def tile_blockdiagonalgru_kernel(tc, x, h, W_ih, W_hh, b_ih, b_hh, out):
                     n, ju, step = pending[cursor[0]]
                     cursor[0] = cursor[0] + 1
                     blend(n, ju, step)
-                    if ju == 1 and step == 2:
+                    if ju == 1 and step == 1:
                         blended.append(n)
 
         def load_block(n):

@@ -18,10 +18,14 @@ BATCH = 256
 FLOPS = 2 * BATCH * (3 * K) * K * NB * 2
 
 MANUAL = True
-EV_R = "sssv"
-EV_Z = "ssss"
-EV_N = "sssv"
-EV_A = "vvss"
+ADD_ON_PE = True
+SLOTS = 8
+MX_PER_SLOT = 3
+BLENDS_IN_SLOT = (0, 1, 0, 1, 0, 1, 0, 1)
+V_EVACS_IN_SLOT = (0, 0, 1, 0, 1, 1, 1, 0)
+W_CHUNKS = ((0, 0), (1, 0), (1, 2), (0, 2), (0, 1), (1, 1))
+Q_LAG = 2
+WHEN = {"sig0": (6, 7), "mul": (8, 9), "add": (10, 11), "tanh": (11, 16), "sig1": (12, 13)}
 
 
 def tile_blockdiagonalgru_kernel(tc, x, h, W_ih, W_hh, b_ih, b_hh, out):
@@ -30,7 +34,7 @@ def tile_blockdiagonalgru_kernel(tc, x, h, W_ih, W_hh, b_ih, b_hh, out):
         const = ctx.enter_context(tc.tile_pool(name="const", bufs=1))
         wpool = ctx.enter_context(tc.tile_pool(name="wpool", bufs=3))
         grp = ctx.enter_context(tc.tile_pool(name="grp", bufs=4))
-        cod = ctx.enter_context(tc.tile_pool(name="cod", bufs=4))
+        cod = ctx.enter_context(tc.tile_pool(name="cod", bufs=8))
         epi = ctx.enter_context(tc.tile_pool(name="epi", bufs=2))
         psT = ctx.enter_context(tc.psum_pool(name="psT", bufs=4))
         psM = ctx.enter_context(tc.psum_pool(name="psM", bufs=4))
@@ -81,8 +85,9 @@ def tile_blockdiagonalgru_kernel(tc, x, h, W_ih, W_hh, b_ih, b_hh, out):
                 st["w", n, m] = wpool.tile([P, 6, 2 * K], BF16, name="wraw%d" % m)
             return st["w", n, m]
 
-        def load_w(n, m, s0, s1):
-            nc.sync.dma_start(out=w_tile(n, m)[:, s0:s1, :], in_=w_view[m][n, :, s0:s1, :])
+        def load_block(n):
+            for m, g in W_CHUNKS:
+                nc.sync.dma_start(out=w_tile(n, m)[:, 2 * g:2 * g + 2, :], in_=w_view[m][n, :, 2 * g:2 * g + 2, :])
 
         def prep_bias():
             for m, b in enumerate((b_ih, b_hh)):
@@ -96,7 +101,13 @@ def tile_blockdiagonalgru_kernel(tc, x, h, W_ih, W_hh, b_ih, b_hh, out):
             nc.vector.tensor_copy(out=bias_f[:].rearrange("p m r e -> p (m r e)"), in_=bps[:, 0:2 * P].bitcast(BF16))
             nc.vector.tensor_tensor(out=brz[:], in0=bias_f[:, 0, 0:48, :], in1=bias_f[:, 1, 0:48, :], op=ALU.add)
 
-        def t_chunk(key, srcs):
+        def t_chunk(key):
+            if key[0] == "w":
+                n, m, g = key[1:]
+                ww = w_tile(n, m)[:].bitcast(F32)
+                srcs = [ww[:, g * 2 + t // 2, (t % 2) * 256:(t % 2) * 256 + 256] for t in range(4)]
+            else:
+                srcs = [xh_words[key[1]][q][:, a, :] for q in range(2) for a in range(2)]
             banks = []
             for b in range(2):
                 tp = psT.tile([P, 512], F32, name="tp", tag="T")
@@ -107,17 +118,10 @@ def tile_blockdiagonalgru_kernel(tc, x, h, W_ih, W_hh, b_ih, b_hh, out):
                 banks.append(tp)
             st["tb", key] = banks
 
-        def t_w(n, m, g):
-            ww = w_tile(n, m)[:].bitcast(F32)
-            t_chunk(("w", n, m, g), [ww[:, g * 2 + t // 2, (t % 2) * 256:(t % 2) * 256 + 256] for t in range(4)])
-
-        def t_xh(n):
-            t_chunk(("xh", n), [xh_words[n][q][:, a, :] for q in range(2) for a in range(2)])
-
         def e_bank(key, b, eng):
             if ("g", key) not in st:
                 tag = "gx" if key[0] == "xh" else "gw"
-                st["g", key] = grp.tile([P, 4 * K], BF16, name=tag, bufs=4, align_bytes=64)
+                st["g", key] = grp.tile([P, 4 * K], BF16, name=tag, align_bytes=64)
             g32 = st["g", key][:].bitcast(F32)
             evac(
                 eng,
@@ -125,80 +129,63 @@ def tile_blockdiagonalgru_kernel(tc, x, h, W_ih, W_hh, b_ih, b_hh, out):
                 st["tb", key][b][:].rearrange("p (i v r) -> p i r v", i=2, v=2),
             )
 
-        def q_w(n, m, g):
-            if ("wc", n, g) not in st:
-                st["wc", n, g] = cod.tile([P, 2, 512], U32, name="wc", align_bytes=64)
-                st["ws", n, g] = cod.tile([P, 2, 512], U8, name="ws", align_bytes=64)
-            nc.vector.quantize_mx(
-                out=st["wc", n, g][:, m, :].bitcast(FP8X4), scales=st["ws", n, g][:, m, :], in_=st["g", ("w", n, m, g)][:]
-            )
+        def quantise(key):
+            tag = "x" if key[0] == "xh" else "w"
+            bufs = 3 if key[0] == "xh" else 8
+            st["c", key] = cod.tile([P, 512], U32, name=tag + "c", bufs=bufs, align_bytes=64)
+            st["s", key] = cod.tile([P, 512], U8, name=tag + "s", bufs=bufs, align_bytes=64)
+            nc.vector.quantize_mx(out=st["c", key][:].bitcast(FP8X4), scales=st["s", key][:], in_=st["g", key][:])
 
-        def q_xh(n):
-            st["xc", n] = cod.tile([P, 512], U32, name="xc", bufs=3, align_bytes=64)
-            st["xs", n] = cod.tile([P, 512], U8, name="xs", bufs=3, align_bytes=64)
-            nc.vector.quantize_mx(out=st["xc", n][:].bitcast(FP8X4), scales=st["xs", n][:], in_=st["g", ("xh", n)][:])
-
-        def mx(n, g, m, t, dst, start, stop):
+        def mx_pass(n, g, m, t, start, stop):
+            bkey = ("m", n, g, m if g == 2 else 0, t // 2)
+            if bkey not in st:
+                st[bkey] = psM.tile([P, 512], F32, name="mp", tag="M")
+            wk = ("w", n, m, g)
+            xk = ("xh", n)
             nc.tensor.matmul_mx(
-                out=dst,
-                lhsT=st["wc", n, g][:, m, t * P:(t + 1) * P].bitcast(FP8X4),
-                lhsT_scale=st["ws", n, g][:, m, t * P:(t + 1) * P],
-                rhs=st["xc", n][:, m * BATCH:(m + 1) * BATCH].bitcast(FP8X4),
-                rhs_scale=st["xs", n][:, m * BATCH:(m + 1) * BATCH],
+                out=st[bkey][:, (t % 2) * BATCH:(t % 2 + 1) * BATCH],
+                lhsT=st["c", wk][:, t * P:(t + 1) * P].bitcast(FP8X4),
+                lhsT_scale=st["s", wk][:, t * P:(t + 1) * P],
+                rhs=st["c", xk][:, m * BATCH:(m + 1) * BATCH].bitcast(FP8X4),
+                rhs_scale=st["s", xk][:, m * BATCH:(m + 1) * BATCH],
                 start=start,
                 stop=stop,
             )
 
-        def mx_rz(n, g):
-            banks = []
-            for ju in range(2):
-                mp = psM.tile([P, 512], F32, name="mp", tag="M")
-                for je in range(2):
-                    for m in range(2):
-                        mx(n, g, m, 2 * ju + je, mp[:, je * BATCH:(je + 1) * BATCH], m == 0, m == 1)
-                banks.append(mp)
-            st["m", n, g] = banks
-
-        def mx_n(n, ju):
-            pair = []
-            for m in (1, 0):
-                mp = psM.tile([P, 512], F32, name="mp", tag="M")
-                for je in range(2):
-                    mx(n, 2, m, 2 * ju + je, mp[:, je * BATCH:(je + 1) * BATCH], True, True)
-                pair.append(mp)
-            st["mn", n, ju] = pair
-
-        def sig(n, g):
-            dst = epi.tile([P, 4, BATCH], F32, name="gate%d" % g, bufs=2 + g)
-            st["gate", n, g] = dst
-            for t in range(4):
+        def sig(n, g, ju):
+            if g == 1:
+                st["sigd", n, ju] = True
+            if ("gate", n, g) not in st:
+                st["gate", n, g] = epi.tile([P, 4, BATCH], F32, name="gate%d" % g, bufs=2 + g)
+            for je in range(2):
                 nc.scalar.activation(
-                    out=dst[:, t, :],
-                    in_=st["m", n, g][t // 2][:, (t % 2) * BATCH:(t % 2 + 1) * BATCH],
+                    out=st["gate", n, g][:, 2 * ju + je, :],
+                    in_=st["m", n, g, 0, ju][:, je * BATCH:(je + 1) * BATCH],
                     func=ACT.Sigmoid,
-                    bias=brz[:, n * 6 + g * 2 + t // 2, t % 2:t % 2 + 1],
+                    bias=brz[:, n * 6 + g * 2 + ju, je:je + 1],
                     scale=1.0,
                 )
 
-        def n_pre(n, ju):
-            y = epi.tile([P, 2, BATCH], F32, name="y", bufs=3)
+        def n_mul(n, ju):
+            y = epi.tile([P, 2, BATCH], F32, name="y", bufs=4)
             st["y", n, ju] = y
-            hn, xn = st["mn", n, ju]
             for je in range(2):
                 nc.vector.scalar_tensor_tensor(
                     out=y[:, je, :],
-                    in0=hn[:, je * BATCH:(je + 1) * BATCH],
+                    in0=st["m", n, 2, 1, ju][:, je * BATCH:(je + 1) * BATCH],
                     scalar=bias_f[:, 1, n * 6 + 4 + ju, je:je + 1],
                     in1=st["gate", n, 0][:, 2 * ju + je, :],
                     op0=ALU.add,
                     op1=ALU.mult,
                 )
-            yf = y[:].rearrange("p e b -> p (e b)")
-            nc.vector.tensor_tensor(out=yf, in0=xn[:], in1=yf, op=ALU.add)
+
+        def n_add(n, ju):
+            yf = st["y", n, ju][:].rearrange("p e b -> p (e b)")
+            nc.vector.tensor_tensor(out=yf, in0=st["m", n, 2, 0, ju][:], in1=yf, op=ALU.add)
 
         def n_tanh(n, ju):
             c = epi.tile([P, 2, BATCH], F32, name="c", bufs=6)
-            st["c", n, ju] = c
+            st["cand", n, ju] = c
             for je in range(2):
                 nc.scalar.activation(
                     out=c[:, je, :],
@@ -207,73 +194,79 @@ def tile_blockdiagonalgru_kernel(tc, x, h, W_ih, W_hh, b_ih, b_hh, out):
                     bias=bias_f[:, 0, n * 6 + 4 + ju, je:je + 1],
                     scale=1.0,
                 )
-            pending.extend([(n, ju, 0), (n, ju, 1)])
 
         def blend(n, ju, step):
-            c = st["c", n, ju]
+            c = st["cand", n, ju]
             if step == 0:
                 d = epi.tile([P, 2, BATCH], F32, name="d", bufs=6)
                 st["d", n, ju] = d
                 h_t = st["g", ("xh", n)][:, 2 * K:4 * K].rearrange("p (b t) -> p t b", t=4)[:, 2 * ju:2 * ju + 2, :]
                 nc.vector.tensor_tensor(out=d[:], in0=h_t, in1=c[:], op=ALU.subtract)
-            else:
+            elif step == 1:
                 d = st["d", n, ju]
                 nc.vector.tensor_tensor(out=d[:], in0=d[:], in1=st["gate", n, 1][:, 2 * ju:2 * ju + 2, :], op=ALU.mult)
-
+            else:
+                d = st["d", n, ju]
+                nc.vector.tensor_tensor(out=d[:], in0=d[:], in1=c[:], op=ALU.add)
 
         def t_out(n):
             banks = []
             for a in range(2):
                 tp = psT.tile([P, 512], F32, name="tp", tag="T")
                 for t in range(4):
-                    for i, term in enumerate(("c", "d")):
-                        nc.tensor.matmul(
-                            out=tp[:, t * P:(t + 1) * P],
-                            lhsT=st[term, n, t // 2][:, t % 2, a * P:(a + 1) * P],
-                            rhs=ident[:],
-                            start=(i == 0),
-                            stop=(i == 1),
-                            is_transpose=True,
-                        )
+                    dst = tp[:, t * P:(t + 1) * P]
+                    if ADD_ON_PE:
+                        for i, term in enumerate(("cand", "d")):
+                            nc.tensor.matmul(
+                                out=dst,
+                                lhsT=st[term, n, t // 2][:, t % 2, a * P:(a + 1) * P],
+                                rhs=ident[:],
+                                start=(i == 0),
+                                stop=(i == 1),
+                                is_transpose=True,
+                            )
+                    else:
+                        nc.tensor.transpose(dst, st["d", n, t // 2][:, t % 2, a * P:(a + 1) * P], ident[:])
                 banks.append(tp)
             st["ot", n] = banks
+            st["osb", n] = epi.tile([P, 2, K], F32, name="osb")
 
-        def e_out(n, engs):
-            osb = epi.tile([P, 2, K], F32, name="osb")
-            for a in range(2):
-                evac(
-                    engs[a],
-                    osb[:, a, :].rearrange("b (ju p je) -> b ju p je", ju=2, je=2),
-                    st["ot", n][a][:].rearrange("b (ju je p) -> b ju p je", ju=2, je=2),
-                )
-            nc.sync.dma_start(out=out_view[:, :, n * K:(n + 1) * K], in_=osb[:])
+        def e_out(n, a, eng):
+            evac(
+                eng,
+                st["osb", n][:, a, :].rearrange("b (ju p je) -> b ju p je", ju=2, je=2),
+                st["ot", n][a][:].rearrange("b (ju je p) -> b ju p je", ju=2, je=2),
+            )
 
+        def store(n):
+            nc.sync.dma_start(out=out_view[:, :, n * K:(n + 1) * K], in_=st["osb", n][:])
+
+        n_steps = 2 if ADD_ON_PE else 3
+        passes = []
+        for n in range(NB):
+            for t in range(4):
+                passes.append((n, 0, 0, t, True, False))
+                passes.append((n, 0, 1, t, False, True))
+            for m in (1, 0):
+                for t in range(4):
+                    passes.append((n, 2, m, t, True, True))
+            for t in range(4):
+                passes.append((n, 1, 0, t, True, False))
+                passes.append((n, 1, 1, t, False, True))
+        quantised = {}
+        s_todo = {}
+        v_todo = {}
         pending = []
         blended = []
+        cur = [0, 0, 0]
+        banks_open = [0]
+        chunks = {}
 
-        cursor = [0, 0]
-
-        def bl(count=1):
-            for i in range(count):
-                if cursor[0] < len(pending):
-                    n, ju, step = pending[cursor[0]]
-                    cursor[0] = cursor[0] + 1
-                    blend(n, ju, step)
-                    if ju == 1 and step == 1:
-                        blended.append(n)
-
-        def load_block(n):
-            for g in range(3):
-                load_w(n, 0, 2 * g, 2 * g + 2)
-                load_w(n, 1, 2 * g, 2 * g + 2)
-
-        def t_pair(n, g):
-            t_w(n, 0, g)
-            t_w(n, 1, g)
-
-        def e_pair(n, g, banks, engs):
-            for b in banks:
-                e_bank(("w", n, b // 2, g), b % 2, engs[b])
+        def later(todo, slot, kind, n, ju):
+            when = max(slot + 1, n * SLOTS + WHEN[kind][ju]) if n < NB - 1 else slot + 1
+            if when not in todo:
+                todo[when] = []
+            todo[when].append((kind, n, ju))
 
         load_xh(0, 1)
         prep_bias()
@@ -284,75 +277,77 @@ def tile_blockdiagonalgru_kernel(tc, x, h, W_ih, W_hh, b_ih, b_hh, out):
         load_block(2)
         load_xh(4, 8)
 
-        t_xh(0)
-        e_bank(("xh", 0), 0, "s")
-        e_bank(("xh", 0), 1, "v")
-        q_xh(0)
-
-        for n in range(NB + 2):
-            cur = n < NB
-            prev = 1 <= n <= NB
-            if cur:
-                t_pair(n, 0)
-            if prev:
-                n_pre(n - 1, 0)
-            if cur:
-                e_pair(n, 0, (0, 1, 2, 3), EV_R)
-            bl()
-            if cur:
-                q_w(n, 0, 0)
-            bl()
-            if cur:
-                q_w(n, 1, 0)
-            if prev:
-                n_tanh(n - 1, 0)
-                mx_n(n - 1, 1)
-            if cur:
-                t_pair(n, 1)
-            if prev:
-                n_pre(n - 1, 1)
-            if cur:
-                e_pair(n, 1, (0, 1, 2, 3), EV_Z)
-            if prev:
-                n_tanh(n - 1, 1)
-            if cur:
-                mx_rz(n, 0)
-                q_w(n, 0, 1)
-            bl()
-            if cur:
-                q_w(n, 1, 1)
-            bl()
-            if n == 0:
+        for slot in range(-2, SLOTS * NB + 30):
+            n, i = slot // SLOTS, slot % SLOTS
+            tail = slot >= SLOTS * NB - 2
+            chunk = None
+            back = None
+            if slot == 4:
                 bias_transpose()
-            if cur:
-                t_pair(n, 2)
-                if n + 3 < NB:
-                    load_block(n + 3)
-                e_pair(n, 2, (0, 1), EV_N)
-                sig(n, 0)
-                e_pair(n, 2, (2, 3), EV_N)
-                mx_rz(n, 1)
-            bl()
-            if cur:
-                q_w(n, 0, 2)
-            bl()
-            if cur:
-                q_w(n, 1, 2)
-            if n + 1 < NB:
-                t_xh(n + 1)
-            done = blended[cursor[1]:]
-            cursor[1] = len(blended)
-            for m in done:
-                t_out(m)
-            if cur:
-                sig(n, 1)
-            if n + 1 < NB:
-                e_bank(("xh", n + 1), 0, EV_A[0])
-                e_bank(("xh", n + 1), 1, EV_A[1])
-            for m in done:
-                e_out(m, EV_A[2:4])
-            if cur:
-                mx_n(n, 0)
-            bl()
-            if n + 1 < NB:
-                q_xh(n + 1)
+            if slot == -2:
+                chunk = ("xh", 0)
+            elif 0 <= n < NB and i < 6:
+                chunk = ("w", n) + W_CHUNKS[i]
+            elif 0 <= n and n + 1 < NB and i == 6:
+                chunk = ("xh", n + 1)
+            elif (i == 7 or tail) and cur[2] < len(blended):
+                back = blended[cur[2]]
+                cur[2] = cur[2] + 1
+            if chunk is not None:
+                t_chunk(chunk)
+                chunks[slot] = chunk
+            if back is not None:
+                t_out(back)
+            if 0 <= n and i == 5 and n + 3 < NB:
+                load_block(n + 3)
+            for k in range(8 if tail else MX_PER_SLOT):
+                if cur[0] < len(passes):
+                    pn, g, m, t, start, stop = passes[cur[0]]
+                    ready = quantised.get(("w", pn, m, g), slot) < slot and quantised.get(("xh", pn), slot) < slot
+                    if t % 2 == 0 and start and banks_open[0] == 4:
+                        ready = False
+                    if ready:
+                        if t % 2 == 0 and start:
+                            banks_open[0] = banks_open[0] + 1
+                        mx_pass(pn, g, m, t, start, stop)
+                        cur[0] = cur[0] + 1
+                        if t % 2 == 1 and stop:
+                            if g < 2:
+                                later(s_todo, slot, "sig%d" % g, pn, t // 2)
+                            else:
+                                later(v_todo, slot, "mul" if m == 1 else "add", pn, t // 2)
+            for kind, bn, ju in s_todo.get(slot, []):
+                if kind == "tanh":
+                    n_tanh(bn, ju)
+                    for step in range(n_steps):
+                        pending.append((bn, ju, step, slot))
+                else:
+                    sig(bn, 0 if kind == "sig0" else 1, ju)
+                    banks_open[0] = banks_open[0] - 1
+            n_v = 1 if tail else V_EVACS_IN_SLOT[i]
+            if slot - Q_LAG in chunks:
+                quantise(chunks[slot - Q_LAG])
+                quantised[chunks[slot - Q_LAG]] = slot
+            for kind, bn, ju in v_todo.get(slot, []):
+                banks_open[0] = banks_open[0] - 1
+                if kind == "mul":
+                    n_mul(bn, ju)
+                else:
+                    n_add(bn, ju)
+                    later(s_todo, slot, "tanh", bn, ju)
+            for k in range(8 if tail else BLENDS_IN_SLOT[i]):
+                if cur[1] < len(pending) and pending[cur[1]][3] < slot:
+                    bn, ju, step = pending[cur[1]][0:3]
+                    if step != 1 or ("sigd", bn, ju) in st:
+                        cur[1] = cur[1] + 1
+                        blend(bn, ju, step)
+                        if ju == 1 and step == n_steps - 1:
+                            blended.append(bn)
+            for b in range(2):
+                eng = "v" if b >= 2 - n_v else "s"
+                if chunk is not None:
+                    e_bank(chunk, b, eng)
+                if back is not None:
+                    e_out(back, b, eng)
+            if back is not None:
+                store(back)

@@ -20,11 +20,12 @@ FLOPS = 2 * BATCH * (3 * K) * K * NB * 2
 MANUAL = True
 ADD_ON_PE = True
 SLOTS = 8
-MX_PER_SLOT = 3
+MX_PER_SLOT = (3, 3, 3, 3, 3, 3, 3, 3)
 BLENDS_IN_SLOT = (0, 1, 0, 1, 0, 1, 0, 1)
 V_EVACS_IN_SLOT = (0, 0, 1, 0, 1, 1, 1, 0)
 W_CHUNKS = ((0, 0), (1, 0), (1, 2), (0, 2), (0, 1), (1, 1))
 Q_LAG = 2
+FIRST_MX_SLOT = 4
 WHEN = {"sig0": (6, 7), "mul": (8, 9), "add": (10, 11), "tanh": (11, 16), "sig1": (12, 13)}
 
 
@@ -209,37 +210,36 @@ def tile_blockdiagonalgru_kernel(tc, x, h, W_ih, W_hh, b_ih, b_hh, out):
                 d = st["d", n, ju]
                 nc.vector.tensor_tensor(out=d[:], in0=d[:], in1=c[:], op=ALU.add)
 
-        def t_out(n):
-            banks = []
+        def t_out(n, ju):
+            tp = psT.tile([P, 512], F32, name="tp", tag="T")
             for a in range(2):
-                tp = psT.tile([P, 512], F32, name="tp", tag="T")
-                for t in range(4):
-                    dst = tp[:, t * P:(t + 1) * P]
+                for je in range(2):
+                    dst = tp[:, (a * 2 + je) * P:(a * 2 + je + 1) * P]
                     if ADD_ON_PE:
                         for i, term in enumerate(("cand", "d")):
                             nc.tensor.matmul(
                                 out=dst,
-                                lhsT=st[term, n, t // 2][:, t % 2, a * P:(a + 1) * P],
+                                lhsT=st[term, n, ju][:, je, a * P:(a + 1) * P],
                                 rhs=ident[:],
                                 start=(i == 0),
                                 stop=(i == 1),
                                 is_transpose=True,
                             )
                     else:
-                        nc.tensor.transpose(dst, st["d", n, t // 2][:, t % 2, a * P:(a + 1) * P], ident[:])
-                banks.append(tp)
-            st["ot", n] = banks
-            st["osb", n] = epi.tile([P, 2, K], F32, name="osb")
+                        nc.tensor.transpose(dst, st["d", n, ju][:, je, a * P:(a + 1) * P], ident[:])
+            st["ot", n, ju] = tp
+            st["osb", n, ju] = epi.tile([P, 2, 256], F32, name="osb", bufs=4)
 
-        def e_out(n, a, eng):
+        def e_out(n, ju, eng):
             evac(
                 eng,
-                st["osb", n][:, a, :].rearrange("b (ju p je) -> b ju p je", ju=2, je=2),
-                st["ot", n][a][:].rearrange("b (ju je p) -> b ju p je", ju=2, je=2),
+                st["osb", n, ju][:].rearrange("b a (p je) -> b a p je", je=2),
+                st["ot", n, ju][:].rearrange("b (a je p) -> b a p je", a=2, je=2),
             )
 
-        def store(n):
-            nc.sync.dma_start(out=out_view[:, :, n * K:(n + 1) * K], in_=st["osb", n][:])
+        def store(n, ju):
+            c0 = n * K + ju * 256
+            nc.sync.dma_start(out=out_view[:, :, c0:c0 + 256], in_=st["osb", n, ju][:])
 
         n_steps = 2 if ADD_ON_PE else 3
         passes = []
@@ -291,16 +291,22 @@ def tile_blockdiagonalgru_kernel(tc, x, h, W_ih, W_hh, b_ih, b_hh, out):
             elif 0 <= n and n + 1 < NB and i == 6:
                 chunk = ("xh", n + 1)
             elif (i == 7 or tail) and cur[2] < len(blended):
-                back = blended[cur[2]]
-                cur[2] = cur[2] + 1
+                back = blended[cur[2]:cur[2] + 2]
+                if len(back) == 2 and back[0][0] != back[1][0]:
+                    back = back[0:1]
+                if len(back) == 1 and back[0][0] < NB - 1 and back[0][1] == 0:
+                    back = None
+                else:
+                    cur[2] = cur[2] + len(back)
             if chunk is not None:
                 t_chunk(chunk)
                 chunks[slot] = chunk
             if back is not None:
-                t_out(back)
+                for bn, ju in back:
+                    t_out(bn, ju)
             if 0 <= n and i == 5 and n + 3 < NB:
                 load_block(n + 3)
-            for k in range(8 if tail else MX_PER_SLOT):
+            for k in range(8 if tail or slot == FIRST_MX_SLOT else MX_PER_SLOT[i]):
                 if cur[0] < len(passes):
                     pn, g, m, t, start, stop = passes[cur[0]]
                     ready = quantised.get(("w", pn, m, g), slot) < slot and quantised.get(("xh", pn), slot) < slot
@@ -316,7 +322,8 @@ def tile_blockdiagonalgru_kernel(tc, x, h, W_ih, W_hh, b_ih, b_hh, out):
                                 later(s_todo, slot, "sig%d" % g, pn, t // 2)
                             else:
                                 later(v_todo, slot, "mul" if m == 1 else "add", pn, t // 2)
-            for kind, bn, ju in s_todo.get(slot, []):
+            todo = s_todo.get(slot, [])
+            for kind, bn, ju in [op for op in todo if op[0] == "tanh"] + [op for op in todo if op[0] != "tanh"]:
                 if kind == "tanh":
                     n_tanh(bn, ju)
                     for step in range(n_steps):
@@ -341,13 +348,13 @@ def tile_blockdiagonalgru_kernel(tc, x, h, W_ih, W_hh, b_ih, b_hh, out):
                     if step != 1 or ("sigd", bn, ju) in st:
                         cur[1] = cur[1] + 1
                         blend(bn, ju, step)
-                        if ju == 1 and step == n_steps - 1:
-                            blended.append(bn)
+                        if step == n_steps - 1:
+                            blended.append((bn, ju))
             for b in range(2):
                 eng = "v" if b >= 2 - n_v else "s"
                 if chunk is not None:
                     e_bank(chunk, b, eng)
-                if back is not None:
-                    e_out(back, b, eng)
             if back is not None:
-                store(back)
+                for k, (bn, ju) in enumerate(back):
+                    e_out(bn, ju, "v" if k >= 2 - n_v and not tail else "s")
+                    store(bn, ju)

@@ -26,6 +26,8 @@ V_EVACS_IN_SLOT = (0, 0, 1, 0, 1, 1, 1, 0)
 W_CHUNKS = ((0, 0), (1, 0), (1, 2), (0, 2), (0, 1), (1, 1))
 Q_LAG = 2
 FIRST_MX_SLOT = 4
+WARM_FIRST = 6
+WARM_EACH = 1
 WHEN = {"sig0": (6, 7), "mul": (8, 9), "add": (10, 11), "tanh": (11, 16), "sig1": (12, 13)}
 
 
@@ -69,6 +71,14 @@ def tile_blockdiagonalgru_kernel(tc, x, h, W_ih, W_hh, b_ih, b_hh, out):
         brz = const.tile([P, 48, 2], F32, name="brz")
 
         st = {}
+        zeros = const.tile([P, 512], BF16, name="zeros")
+        nc.vector.memset(zeros[:], 0.0)
+
+        def warm(count):
+            if "warm" not in st:
+                st["warm"] = psM.tile([P, 512], F32, name="mp", tag="M")
+            for k in range(count):
+                nc.tensor.matmul(out=st["warm"][:], lhsT=zeros[:, 0:P], rhs=zeros[:], start=True, stop=True)
 
         def evac(eng, dst, src):
             if eng == "s":
@@ -298,9 +308,13 @@ def tile_blockdiagonalgru_kernel(tc, x, h, W_ih, W_hh, b_ih, b_hh, out):
                     back = None
                 else:
                     cur[2] = cur[2] + len(back)
+            if slot == -2:
+                warm(WARM_FIRST)
             if chunk is not None:
                 t_chunk(chunk)
                 chunks[slot] = chunk
+            if slot < FIRST_MX_SLOT:
+                warm(WARM_EACH)
             if back is not None:
                 for bn, ju in back:
                     t_out(bn, ju)

@@ -22,12 +22,10 @@ ADD_ON_PE = True
 SLOTS = 8
 MX_PER_SLOT = (3, 3, 3, 3, 3, 3, 3, 3)
 BLENDS_IN_SLOT = (0, 1, 0, 1, 0, 1, 0, 1)
-V_EVACS_IN_SLOT = (0, 0, 1, 0, 1, 1, 1, 0)
+V_EVACS_IN_SLOT = (0, 0, 0, 0, 1, 1, 1, 0)
 W_CHUNKS = ((0, 0), (1, 0), (1, 2), (0, 2), (0, 1), (1, 1))
 Q_LAG = 2
 FIRST_MX_SLOT = 4
-WARM_FIRST = 6
-WARM_EACH = 1
 WHEN = {"sig0": (6, 7), "mul": (8, 9), "add": (10, 11), "tanh": (11, 16), "sig1": (12, 13)}
 
 
@@ -71,14 +69,6 @@ def tile_blockdiagonalgru_kernel(tc, x, h, W_ih, W_hh, b_ih, b_hh, out):
         brz = const.tile([P, 48, 2], F32, name="brz")
 
         st = {}
-        zeros = const.tile([P, 512], BF16, name="zeros")
-        nc.vector.memset(zeros[:], 0.0)
-
-        def warm(count):
-            if "warm" not in st:
-                st["warm"] = psM.tile([P, 512], F32, name="mp", tag="M")
-            for k in range(count):
-                nc.tensor.matmul(out=st["warm"][:], lhsT=zeros[:, 0:P], rhs=zeros[:], start=True, stop=True)
 
         def evac(eng, dst, src):
             if eng == "s":
@@ -308,13 +298,9 @@ def tile_blockdiagonalgru_kernel(tc, x, h, W_ih, W_hh, b_ih, b_hh, out):
                     back = None
                 else:
                     cur[2] = cur[2] + len(back)
-            if slot == -2:
-                warm(WARM_FIRST)
             if chunk is not None:
                 t_chunk(chunk)
                 chunks[slot] = chunk
-            if slot < FIRST_MX_SLOT:
-                warm(WARM_EACH)
             if back is not None:
                 for bn, ju in back:
                     t_out(bn, ju)

@@ -25,6 +25,7 @@ BLENDS_IN_SLOT = (0, 1, 0, 1, 0, 1, 0, 1)
 V_EVACS_IN_SLOT = (0, 0, 0, 0, 1, 1, 1, 0)
 W_CHUNKS = ((0, 0), (1, 0), (1, 2), (0, 2), (0, 1), (1, 1))
 Q_LAG = 2
+W_AHEAD = 2
 FIRST_MX_SLOT = 4
 WHEN = {"sig0": (6, 7), "mul": (8, 9), "add": (10, 11), "tanh": (11, 16), "sig1": (12, 13)}
 
@@ -33,7 +34,7 @@ def tile_blockdiagonalgru_kernel(tc, x, h, W_ih, W_hh, b_ih, b_hh, out):
     nc = tc.nc
     with ExitStack() as ctx:
         const = ctx.enter_context(tc.tile_pool(name="const", bufs=1))
-        wpool = ctx.enter_context(tc.tile_pool(name="wpool", bufs=3))
+        wpool = ctx.enter_context(tc.tile_pool(name="wpool", bufs=W_AHEAD))
         grp = ctx.enter_context(tc.tile_pool(name="grp", bufs=4))
         cod = ctx.enter_context(tc.tile_pool(name="cod", bufs=8))
         epi = ctx.enter_context(tc.tile_pool(name="epi", bufs=2))
@@ -52,6 +53,9 @@ def tile_blockdiagonalgru_kernel(tc, x, h, W_ih, W_hh, b_ih, b_hh, out):
 
         ident = const.tile([P, P], F32, name="ident")
         make_identity(nc, ident[:])
+        dummy = const.tile([P, 1], F32, name="dummy")
+        nc.vector.memset(dummy[:], 0.0)
+        nc.scalar.activation(out=dummy[:], in_=dummy[:], func=ACT.Sigmoid)
         groups = [(0, 1), (1, 2), (2, 4), (4, 8)]
         xh_raw = {}
         xh_words = {}
@@ -81,14 +85,14 @@ def tile_blockdiagonalgru_kernel(tc, x, h, W_ih, W_hh, b_ih, b_hh, out):
             nc.sync.dma_start(out=xh_raw[n0][0][:], in_=x_view[:, :, cols])
             nc.sync.dma_start(out=xh_raw[n0][1][:], in_=h_view[:, :, cols])
 
-        def w_tile(n, m):
-            if ("w", n, m) not in st:
-                st["w", n, m] = wpool.tile([P, 6, 2 * K], BF16, name="wraw%d" % m)
-            return st["w", n, m]
+        def load_w(n, m, g):
+            raw = wpool.tile([P, 2, 2 * K], BF16, name="wraw%d%d" % (m, g))
+            st["w", n, m, g] = raw
+            nc.sync.dma_start(out=raw[:], in_=w_view[m][n, :, 2 * g:2 * g + 2, :])
 
         def load_block(n):
             for m, g in W_CHUNKS:
-                nc.sync.dma_start(out=w_tile(n, m)[:, 2 * g:2 * g + 2, :], in_=w_view[m][n, :, 2 * g:2 * g + 2, :])
+                load_w(n, m, g)
 
         def prep_bias():
             for m, b in enumerate((b_ih, b_hh)):
@@ -105,8 +109,8 @@ def tile_blockdiagonalgru_kernel(tc, x, h, W_ih, W_hh, b_ih, b_hh, out):
         def t_chunk(key):
             if key[0] == "w":
                 n, m, g = key[1:]
-                ww = w_tile(n, m)[:].bitcast(F32)
-                srcs = [ww[:, g * 2 + t // 2, (t % 2) * 256:(t % 2) * 256 + 256] for t in range(4)]
+                ww = st["w", n, m, g][:].bitcast(F32)
+                srcs = [ww[:, t // 2, (t % 2) * 256:(t % 2) * 256 + 256] for t in range(4)]
             else:
                 srcs = [xh_words[key[1]][q][:, a, :] for q in range(2) for a in range(2)]
             banks = []
@@ -274,8 +278,6 @@ def tile_blockdiagonalgru_kernel(tc, x, h, W_ih, W_hh, b_ih, b_hh, out):
         load_xh(1, 2)
         load_block(1)
         load_xh(2, 4)
-        load_block(2)
-        load_xh(4, 8)
 
         for slot in range(-2, SLOTS * NB + 30):
             n, i = slot // SLOTS, slot % SLOTS
@@ -304,8 +306,10 @@ def tile_blockdiagonalgru_kernel(tc, x, h, W_ih, W_hh, b_ih, b_hh, out):
             if back is not None:
                 for bn, ju in back:
                     t_out(bn, ju)
-            if 0 <= n and i == 5 and n + 3 < NB:
-                load_block(n + 3)
+            if slot == 2 * SLOTS:
+                load_xh(4, 8)
+            if chunk is not None and chunk[0] == "w" and n + W_AHEAD < NB:
+                load_w(n + W_AHEAD, chunk[2], chunk[3])
             for k in range(8 if tail or slot == FIRST_MX_SLOT else MX_PER_SLOT[i]):
                 if cur[0] < len(passes):
                     pn, g, m, t, start, stop = passes[cur[0]]

@@ -18,9 +18,8 @@ BATCH = 256
 FLOPS = 2 * BATCH * (3 * K) * K * NB * 2
 
 MANUAL = True
-ADD_ON_PE = True
 SLOTS = 8
-MX_PER_SLOT = (3, 3, 3, 3, 3, 3, 3, 3)
+MX_PER_SLOT = (0, 4, 4, 4, 4, 4, 4, 0)
 BLENDS_IN_SLOT = (0, 1, 0, 1, 0, 1, 0, 1)
 V_EVACS_IN_SLOT = (0, 0, 0, 0, 1, 1, 1, 0)
 W_CHUNKS = ((0, 0), (1, 0), (1, 2), (0, 2), (0, 1), (1, 1))
@@ -53,6 +52,7 @@ def tile_blockdiagonalgru_kernel(tc, x, h, W_ih, W_hh, b_ih, b_hh, out):
 
         ident = const.tile([P, P], F32, name="ident")
         make_identity(nc, ident[:])
+        ident_h = const.tile([P, P], BF16, name="ident_h")
         dummy = const.tile([P, 1], F32, name="dummy")
         nc.vector.memset(dummy[:], 0.0)
         nc.scalar.activation(out=dummy[:], in_=dummy[:], func=ACT.Sigmoid)
@@ -100,6 +100,7 @@ def tile_blockdiagonalgru_kernel(tc, x, h, W_ih, W_hh, b_ih, b_hh, out):
                 nc.scalar.dma_start(out=braw[m][0:48, :], in_=b.rearrange("n (s w) -> (n s) w", w=256))
 
         def bias_transpose():
+            nc.vector.tensor_copy(out=ident_h[:], in_=ident[:])
             bps = psT.tile([P, 512], F32, name="tp", tag="T")
             for m in range(2):
                 nc.tensor.transpose(bps[:, m * P:(m + 1) * P], braw[m][:].bitcast(F32), ident[:])
@@ -207,30 +208,38 @@ def tile_blockdiagonalgru_kernel(tc, x, h, W_ih, W_hh, b_ih, b_hh, out):
                 st["d", n, ju] = d
                 h_t = st["g", ("xh", n)][:, 2 * K:4 * K].rearrange("p (b t) -> p t b", t=4)[:, 2 * ju:2 * ju + 2, :]
                 nc.vector.tensor_tensor(out=d[:], in0=h_t, in1=c[:], op=ALU.subtract)
-            elif step == 1:
-                d = st["d", n, ju]
-                nc.vector.tensor_tensor(out=d[:], in0=d[:], in1=st["gate", n, 1][:, 2 * ju:2 * ju + 2, :], op=ALU.mult)
             else:
                 d = st["d", n, ju]
-                nc.vector.tensor_tensor(out=d[:], in0=d[:], in1=c[:], op=ALU.add)
+                nc.vector.scalar_tensor_tensor(
+                    out=d[:],
+                    in0=st["gate", n, 1][:, 2 * ju:2 * ju + 2, :],
+                    scalar=1.0,
+                    in1=d[:],
+                    op0=ALU.subtract,
+                    op1=ALU.mult,
+                )
 
         def t_out(n, ju):
             tp = psT.tile([P, 512], F32, name="tp", tag="T")
+            n0 = [g for g in groups if g[0] <= n < g[1]][0][0]
+            c0 = (n - n0) * K + ju * 256
+            nc.tensor.matmul(
+                out=tp[:],
+                lhsT=ident_h[:],
+                rhs=xh_raw[n0][1][:, :, c0:c0 + 256].rearrange("b a (p je) -> b a je p", je=2),
+                start=True,
+                stop=False,
+            )
             for a in range(2):
                 for je in range(2):
-                    dst = tp[:, (a * 2 + je) * P:(a * 2 + je + 1) * P]
-                    if ADD_ON_PE:
-                        for i, term in enumerate(("cand", "d")):
-                            nc.tensor.matmul(
-                                out=dst,
-                                lhsT=st[term, n, ju][:, je, a * P:(a + 1) * P],
-                                rhs=ident[:],
-                                start=(i == 0),
-                                stop=(i == 1),
-                                is_transpose=True,
-                            )
-                    else:
-                        nc.tensor.transpose(dst, st["d", n, ju][:, je, a * P:(a + 1) * P], ident[:])
+                    nc.tensor.matmul(
+                        out=tp[:, (a * 2 + je) * P:(a * 2 + je + 1) * P],
+                        lhsT=st["d", n, ju][:, je, a * P:(a + 1) * P],
+                        rhs=ident[:],
+                        start=False,
+                        stop=(a == 1 and je == 1),
+                        is_transpose=True,
+                    )
             st["ot", n, ju] = tp
             st["osb", n, ju] = epi.tile([P, 2, 256], F32, name="osb", bufs=4)
 
@@ -245,7 +254,7 @@ def tile_blockdiagonalgru_kernel(tc, x, h, W_ih, W_hh, b_ih, b_hh, out):
             c0 = n * K + ju * 256
             nc.sync.dma_start(out=out_view[:, :, c0:c0 + 256], in_=st["osb", n, ju][:])
 
-        n_steps = 2 if ADD_ON_PE else 3
+        n_steps = 2
         passes = []
         for n in range(NB):
             for t in range(4):

from contextlib import ExitStack

import concourse.mybir as mybir
from concourse.masks import make_identity

F32 = mybir.dt.float32
BF16 = mybir.dt.bfloat16
U32 = mybir.dt.uint32
U8 = mybir.dt.uint8
FP8X4 = mybir.dt.float8_e4m3fn_x4
ACT = mybir.ActivationFunctionType
ALU = mybir.AluOpType

P = 128
NB = 8
K = 512
BATCH = 256
FLOPS = 2 * BATCH * (3 * K) * K * NB * 2

MANUAL = True
SLOTS = 8
MX_PER_SLOT = (0, 4, 4, 4, 4, 4, 4, 0)
BLENDS_IN_SLOT = (0, 1, 0, 1, 0, 1, 0, 1)
V_EVACS_IN_SLOT = (0, 0, 0, 0, 1, 1, 1, 0)
W_CHUNKS = ((0, 0), (1, 0), (1, 2), (0, 2), (0, 1), (1, 1))
Q_LAG = 2
W_AHEAD = 2
FIRST_MX_SLOT = 4
WHEN = {"sig0": (6, 7), "mul": (8, 9), "add": (10, 11), "tanh": (11, 16), "sig1": (12, 13)}


def tile_blockdiagonalgru_kernel(tc, x, h, W_ih, W_hh, b_ih, b_hh, out):
    nc = tc.nc
    with ExitStack() as ctx:
        const = ctx.enter_context(tc.tile_pool(name="const", bufs=1))
        wpool = ctx.enter_context(tc.tile_pool(name="wpool", bufs=W_AHEAD))
        grp = ctx.enter_context(tc.tile_pool(name="grp", bufs=4))
        cod = ctx.enter_context(tc.tile_pool(name="cod", bufs=8))
        epi = ctx.enter_context(tc.tile_pool(name="epi", bufs=2))
        psT = ctx.enter_context(tc.psum_pool(name="psT", bufs=4))
        psM = ctx.enter_context(tc.psum_pool(name="psM", bufs=4))
        if MANUAL:
            ctx.enter_context(tc.manual_schedule())

        x_view = x.rearrange("(a p) c -> p a c", p=P)
        h_view = h.rearrange("(a p) c -> p a c", p=P)
        out_view = out.rearrange("(a b) c -> b a c", b=P)
        w_view = [
            W_ih.rearrange("n (s p e) k -> n p s (e k)", p=P, e=2),
            W_hh.rearrange("n (s p e) k -> n p s (e k)", p=P, e=2),
        ]

        ident = const.tile([P, P], F32, name="ident")
        make_identity(nc, ident[:])
        ident_h = const.tile([P, P], BF16, name="ident_h")
        dummy = const.tile([P, 1], F32, name="dummy")
        nc.vector.memset(dummy[:], 0.0)
        nc.scalar.activation(out=dummy[:], in_=dummy[:], func=ACT.Sigmoid)
        groups = [(0, 1), (1, 2), (2, 4), (4, 8)]
        xh_raw = {}
        xh_words = {}
        for n0, n1 in groups:
            xt = const.tile([P, 2, (n1 - n0) * K], BF16, name="x%d" % n0)
            ht = const.tile([P, 2, (n1 - n0) * K], BF16, name="h%d" % n0)
            xh_raw[n0] = (xt, ht)
            for n in range(n0, n1):
                xh_words[n] = [
                    xt[:].bitcast(F32)[:, :, (n - n0) * 256:(n - n0 + 1) * 256],
                    ht[:].bitcast(F32)[:, :, (n - n0) * 256:(n - n0 + 1) * 256],
                ]
        braw = [const.tile([P, 256], BF16, name="braw%d" % m) for m in range(2)]
        bias_f = const.tile([P, 2, P, 2], F32, name="bias_f")
        brz = const.tile([P, 48, 2], F32, name="brz")

        st = {}

        def evac(eng, dst, src):
            if eng == "s":
                nc.scalar.copy(out=dst, in_=src)
            else:
                nc.vector.tensor_copy(out=dst, in_=src)

        def load_xh(n0, n1):
            cols = slice(n0 * K, n1 * K)
            nc.sync.dma_start(out=xh_raw[n0][0][:], in_=x_view[:, :, cols])
            nc.sync.dma_start(out=xh_raw[n0][1][:], in_=h_view[:, :, cols])

        def load_w(n, m, g):
            raw = wpool.tile([P, 2, 2 * K], BF16, name="wraw%d%d" % (m, g))
            st["w", n, m, g] = raw
            nc.sync.dma_start(out=raw[:], in_=w_view[m][n, :, 2 * g:2 * g + 2, :])

        def load_block(n):
            for m, g in W_CHUNKS:
                load_w(n, m, g)

        def prep_bias():
            for m, b in enumerate((b_ih, b_hh)):
                nc.vector.memset(braw[m][:], 0.0)
                nc.scalar.dma_start(out=braw[m][0:48, :], in_=b.rearrange("n (s w) -> (n s) w", w=256))

        def bias_transpose():
            nc.vector.tensor_copy(out=ident_h[:], in_=ident[:])
            bps = psT.tile([P, 512], F32, name="tp", tag="T")
            for m in range(2):
                nc.tensor.transpose(bps[:, m * P:(m + 1) * P], braw[m][:].bitcast(F32), ident[:])
            nc.vector.tensor_copy(out=bias_f[:].rearrange("p m r e -> p (m r e)"), in_=bps[:, 0:2 * P].bitcast(BF16))
            nc.vector.tensor_tensor(out=brz[:], in0=bias_f[:, 0, 0:48, :], in1=bias_f[:, 1, 0:48, :], op=ALU.add)

        def t_chunk(key):
            if key[0] == "w":
                n, m, g = key[1:]
                ww = st["w", n, m, g][:].bitcast(F32)
                srcs = [ww[:, t // 2, (t % 2) * 256:(t % 2) * 256 + 256] for t in range(4)]
            else:
                srcs = [xh_words[key[1]][q][:, a, :] for q in range(2) for a in range(2)]
            banks = []
            for b in range(2):
                tp = psT.tile([P, 512], F32, name="tp", tag="T")
                for i in range(2):
                    for kv in range(2):
                        c0 = (i * 2 + kv) * P
                        nc.tensor.transpose(tp[:, c0:c0 + P], srcs[2 * b + i][:, kv * P:(kv + 1) * P], ident[:])
                banks.append(tp)
            st["tb", key] = banks

        def e_bank(key, b, eng):
            if ("g", key) not in st:
                tag = "gx" if key[0] == "xh" else "gw"
                st["g", key] = grp.tile([P, 4 * K], BF16, name=tag, align_bytes=64)
            g32 = st["g", key][:].bitcast(F32)
            evac(
                eng,
                g32[:, b * 512:(b + 1) * 512].rearrange("p (i r v) -> p i r v", i=2, v=2),
                st["tb", key][b][:].rearrange("p (i v r) -> p i r v", i=2, v=2),
            )

        def quantise(key):
            tag = "x" if key[0] == "xh" else "w"
            bufs = 3 if key[0] == "xh" else 8
            st["c", key] = cod.tile([P, 512], U32, name=tag + "c", bufs=bufs, align_bytes=64)
            st["s", key] = cod.tile([P, 512], U8, name=tag + "s", bufs=bufs, align_bytes=64)
            nc.vector.quantize_mx(out=st["c", key][:].bitcast(FP8X4), scales=st["s", key][:], in_=st["g", key][:])

        def mx_pass(n, g, m, t, start, stop):
            bkey = ("m", n, g, m if g == 2 else 0, t // 2)
            if bkey not in st:
                st[bkey] = psM.tile([P, 512], F32, name="mp", tag="M")
            wk = ("w", n, m, g)
            xk = ("xh", n)
            nc.tensor.matmul_mx(
                out=st[bkey][:, (t % 2) * BATCH:(t % 2 + 1) * BATCH],
                lhsT=st["c", wk][:, t * P:(t + 1) * P].bitcast(FP8X4),
                lhsT_scale=st["s", wk][:, t * P:(t + 1) * P],
                rhs=st["c", xk][:, m * BATCH:(m + 1) * BATCH].bitcast(FP8X4),
                rhs_scale=st["s", xk][:, m * BATCH:(m + 1) * BATCH],
                start=start,
                stop=stop,
            )

        def sig(n, g, ju):
            if g == 1:
                st["sigd", n, ju] = True
            if ("gate", n, g) not in st:
                st["gate", n, g] = epi.tile([P, 4, BATCH], F32, name="gate%d" % g, bufs=2 + g)
            for je in range(2):
                nc.scalar.activation(
                    out=st["gate", n, g][:, 2 * ju + je, :],
                    in_=st["m", n, g, 0, ju][:, je * BATCH:(je + 1) * BATCH],
                    func=ACT.Sigmoid,
                    bias=brz[:, n * 6 + g * 2 + ju, je:je + 1],
                    scale=1.0,
                )

        def n_mul(n, ju):
            y = epi.tile([P, 2, BATCH], F32, name="y", bufs=4)
            st["y", n, ju] = y
            for je in range(2):
                nc.vector.scalar_tensor_tensor(
                    out=y[:, je, :],
                    in0=st["m", n, 2, 1, ju][:, je * BATCH:(je + 1) * BATCH],
                    scalar=bias_f[:, 1, n * 6 + 4 + ju, je:je + 1],
                    in1=st["gate", n, 0][:, 2 * ju + je, :],
                    op0=ALU.add,
                    op1=ALU.mult,
                )

        def n_add(n, ju):
            yf = st["y", n, ju][:].rearrange("p e b -> p (e b)")
            nc.vector.tensor_tensor(out=yf, in0=st["m", n, 2, 0, ju][:], in1=yf, op=ALU.add)

        def n_tanh(n, ju):
            c = epi.tile([P, 2, BATCH], F32, name="c", bufs=6)
            st["cand", n, ju] = c
            for je in range(2):
                nc.scalar.activation(
                    out=c[:, je, :],
                    in_=st["y", n, ju][:, je, :],
                    func=ACT.Tanh,
                    bias=bias_f[:, 0, n * 6 + 4 + ju, je:je + 1],
                    scale=1.0,
                )

        def blend(n, ju, step):
            c = st["cand", n, ju]
            if step == 0:
                d = epi.tile([P, 2, BATCH], F32, name="d", bufs=6)
                st["d", n, ju] = d
                h_t = st["g", ("xh", n)][:, 2 * K:4 * K].rearrange("p (b t) -> p t b", t=4)[:, 2 * ju:2 * ju + 2, :]
                nc.vector.tensor_tensor(out=d[:], in0=h_t, in1=c[:], op=ALU.subtract)
            else:
                d = st["d", n, ju]
                nc.vector.scalar_tensor_tensor(
                    out=d[:],
                    in0=st["gate", n, 1][:, 2 * ju:2 * ju + 2, :],
                    scalar=1.0,
                    in1=d[:],
                    op0=ALU.subtract,
                    op1=ALU.mult,
                )

        def t_out(n, ju):
            tp = psT.tile([P, 512], F32, name="tp", tag="T")
            n0 = [g for g in groups if g[0] <= n < g[1]][0][0]
            c0 = (n - n0) * K + ju * 256
            nc.tensor.matmul(
                out=tp[:],
                lhsT=ident_h[:],
                rhs=xh_raw[n0][1][:, :, c0:c0 + 256].rearrange("b a (p je) -> b a je p", je=2),
                start=True,
                stop=False,
            )
            for a in range(2):
                for je in range(2):
                    nc.tensor.matmul(
                        out=tp[:, (a * 2 + je) * P:(a * 2 + je + 1) * P],
                        lhsT=st["d", n, ju][:, je, a * P:(a + 1) * P],
                        rhs=ident[:],
                        start=False,
                        stop=(a == 1 and je == 1),
                        is_transpose=True,
                    )
            st["ot", n, ju] = tp
            st["osb", n, ju] = epi.tile([P, 2, 256], F32, name="osb", bufs=4)

        def e_out(n, ju, eng):
            evac(
                eng,
                st["osb", n, ju][:].rearrange("b a (p je) -> b a p je", je=2),
                st["ot", n, ju][:].rearrange("b (a je p) -> b a p je", a=2, je=2),
            )

        def store(n, ju):
            c0 = n * K + ju * 256
            nc.sync.dma_start(out=out_view[:, :, c0:c0 + 256], in_=st["osb", n, ju][:])

        n_steps = 2
        passes = []
        for n in range(NB):
            for t in range(4):
                passes.append((n, 0, 0, t, True, False))
                passes.append((n, 0, 1, t, False, True))
            for m in (1, 0):
                for t in range(4):
                    passes.append((n, 2, m, t, True, True))
            for t in range(4):
                passes.append((n, 1, 0, t, True, False))
                passes.append((n, 1, 1, t, False, True))
        quantised = {}
        s_todo = {}
        v_todo = {}
        pending = []
        blended = []
        cur = [0, 0, 0]
        banks_open = [0]
        chunks = {}

        def later(todo, slot, kind, n, ju):
            when = max(slot + 1, n * SLOTS + WHEN[kind][ju]) if n < NB - 1 else slot + 1
            if when not in todo:
                todo[when] = []
            todo[when].append((kind, n, ju))

        load_xh(0, 1)
        prep_bias()
        load_block(0)
        load_xh(1, 2)
        load_block(1)
        load_xh(2, 4)

        for slot in range(-2, SLOTS * NB + 30):
            n, i = slot // SLOTS, slot % SLOTS
            tail = slot >= SLOTS * NB - 2
            chunk = None
            back = None
            if slot == 4:
                bias_transpose()
            if slot == -2:
                chunk = ("xh", 0)
            elif 0 <= n < NB and i < 6:
                chunk = ("w", n) + W_CHUNKS[i]
            elif 0 <= n and n + 1 < NB and i == 6:
                chunk = ("xh", n + 1)
            elif (i == 7 or tail) and cur[2] < len(blended):
                back = blended[cur[2]:cur[2] + 2]
                if len(back) == 2 and back[0][0] != back[1][0]:
                    back = back[0:1]
                if len(back) == 1 and back[0][0] < NB - 1 and back[0][1] == 0:
                    back = None
                else:
                    cur[2] = cur[2] + len(back)
            if chunk is not None:
                t_chunk(chunk)
                chunks[slot] = chunk
            if back is not None:
                for bn, ju in back:
                    t_out(bn, ju)
            if slot == 2 * SLOTS:
                load_xh(4, 8)
            if chunk is not None and chunk[0] == "w" and n + W_AHEAD < NB:
                load_w(n + W_AHEAD, chunk[2], chunk[3])
            for k in range(8 if tail or slot == FIRST_MX_SLOT else MX_PER_SLOT[i]):
                if cur[0] < len(passes):
                    pn, g, m, t, start, stop = passes[cur[0]]
                    ready = quantised.get(("w", pn, m, g), slot) < slot and quantised.get(("xh", pn), slot) < slot
                    if t % 2 == 0 and start and banks_open[0] == 4:
                        ready = False
                    if ready:
                        if t % 2 == 0 and start:
                            banks_open[0] = banks_open[0] + 1
                        mx_pass(pn, g, m, t, start, stop)
                        cur[0] = cur[0] + 1
                        if t % 2 == 1 and stop:
                            if g < 2:
                                later(s_todo, slot, "sig%d" % g, pn, t // 2)
                            else:
                                later(v_todo, slot, "mul" if m == 1 else "add", pn, t // 2)
            todo = s_todo.get(slot, [])
            for kind, bn, ju in [op for op in todo if op[0] == "tanh"] + [op for op in todo if op[0] != "tanh"]:
                if kind == "tanh":
                    n_tanh(bn, ju)
                    for step in range(n_steps):
                        pending.append((bn, ju, step, slot))
                else:
                    sig(bn, 0 if kind == "sig0" else 1, ju)
                    banks_open[0] = banks_open[0] - 1
            n_v = 1 if tail else V_EVACS_IN_SLOT[i]
            if slot - Q_LAG in chunks:
                quantise(chunks[slot - Q_LAG])
                quantised[chunks[slot - Q_LAG]] = slot
            for kind, bn, ju in v_todo.get(slot, []):
                banks_open[0] = banks_open[0] - 1
                if kind == "mul":
                    n_mul(bn, ju)
                else:
                    n_add(bn, ju)
                    later(s_todo, slot, "tanh", bn, ju)
            for k in range(8 if tail else BLENDS_IN_SLOT[i]):
                if cur[1] < len(pending) and pending[cur[1]][3] < slot:
                    bn, ju, step = pending[cur[1]][0:3]
                    if step != 1 or ("sigd", bn, ju) in st:
                        cur[1] = cur[1] + 1
                        blend(bn, ju, step)
                        if step == n_steps - 1:
                            blended.append((bn, ju))
            for b in range(2):
                eng = "v" if b >= 2 - n_v else "s"
                if chunk is not None:
                    e_bank(chunk, b, eng)
            if back is not None:
                for k, (bn, ju) in enumerate(back):
                    e_out(bn, ju, "v" if k >= 2 - n_v and not tail else "s")
                    store(bn, ju)
